import numpy as np
import ml_dtypes


def mxq(x, axis, fmt="e4m3"):
    dtype, down = {"e4m3": (ml_dtypes.float8_e4m3fn, 7), "e5m2": (ml_dtypes.float8_e5m2, 14)}[fmt]
    v = np.moveaxis(np.asarray(x, np.float32).astype(ml_dtypes.bfloat16).astype(np.float64), axis, -1)
    blocks = v.reshape(v.shape[:-1] + (-1, 32))
    amax = np.abs(blocks).max(-1, keepdims=True)
    byte = np.maximum(np.where(amax > 0, np.frexp(amax)[1] - 1 + 127, 0) - down, 1)
    scale = np.exp2(byte - 127.0)
    codes = (blocks / scale).astype(np.float32).astype(dtype).astype(np.float64)
    return np.moveaxis((codes * scale).reshape(v.shape), -1, axis)


WIDE = False


def mx_kscale(k):
    if not WIDE:
        return np.ones(k)
    levels = np.array([10, -10, 5, -5, 0])
    a = np.random.permutation(np.resize(levels, k // 512 * 4)).reshape(k // 512, 4)
    idx = np.arange(k)
    return np.exp2(a[idx // 512, idx % 128 // 32])


BF16 = ml_dtypes.bfloat16


def bf(x):
    return np.asarray(x, np.float32).astype(BF16)


def f64(x):
    return np.asarray(x).astype(np.float64)


N = 1536


def setup_inputs():
    s = mx_kscale(N)
    return {"A": bf(np.random.standard_normal((N, N)) * s), "B": bf(np.random.standard_normal((N, N)) * 1.5 / np.sqrt(N) / s[:, None])}


def reference(A, B):
    C = mxq(np.triu(f64(A)), 1, "e4m3") @ mxq(np.triu(f64(B)), 0, "e4m3")
    return np.triu(C)

@@ -1,0 +1,248 @@
+from contextlib import ExitStack
+
+import concourse.mybir as mybir
+from concourse.masks import make_identity
+
+FP8X4 = mybir.dt.float8_e4m3fn_x4
+BF16 = mybir.dt.bfloat16
+F32 = mybir.dt.float32
+I32 = mybir.dt.int32
+U32 = mybir.dt.uint32
+U8 = mybir.dt.uint8
+ALU = mybir.AluOpType
+
+N = 1536
+P = 128
+KP = 512
+NG = N // KP
+
+FLOPS = 2 * N * (N + 1) * (N + 2) // 6
+BYTES = 2 * (N * (N + 1) // 2) * 2 + N * N * 4
+
+PIECES = {0: [(0, 512)], 1: [(128, 128), (256, 256)], 2: [(256, 256)], 3: [(384, 128)]}
+
+
+def slot(first, second):
+    base = {2: 0, 1: 1, 0: 3}
+    return base[first] + second - first
+
+
+def tile_modelnew_kernel(tc, A, B, out):
+    nc = tc.nc
+    with ExitStack() as ctx:
+        const = ctx.enter_context(tc.tile_pool(name="const", bufs=1))
+        keep = ctx.enter_context(tc.tile_pool(name="keep", bufs=1))
+        psum = ctx.enter_context(tc.psum_pool(name="psum", bufs=1))
+        ctx.enter_context(tc.manual_schedule())
+
+        a_sb = {}
+        o_sb = {}
+        for i in range(12):
+            a_sb[i] = keep.tile([P, N - KP * (i // 4)], BF16, name="a_sb%d" % i)
+            o_sb[i] = keep.tile([P, N], F32, name="o_sb%d" % i)
+        b_raw = {}
+        for c in range(NG):
+            b_raw[c] = keep.tile([P, 4, N - KP * c], BF16, name="b_raw%d" % c)
+        ga = {}
+        gb = {}
+        for s in range(6):
+            ga[s] = keep.tile([P, 4 * KP], BF16, name="ga%d" % s, align_bytes=64)
+            gb[s] = keep.tile([P, KP, 4], BF16, name="gb%d" % s, align_bytes=64)
+        a_cod = keep.tile([P, 6, KP], U32, name="a_cod", align_bytes=64)
+        a_scl = keep.tile([P, 6, KP], U8, name="a_scl", align_bytes=64)
+        b_cod = keep.tile([P, 6, KP], U32, name="b_cod", align_bytes=64)
+        b_scl = keep.tile([P, 6, KP], U8, name="b_scl", align_bytes=64)
+        banks = [0]
+
+        def bank(shape):
+            n = banks[0]
+            banks[0] = n + 1
+            return psum.tile(shape, F32, name="bk%d_%d" % (n % 8, n), tag="bk%d" % (n % 8))
+
+        for g in (2, 1, 0):
+            nc.vector.memset(b_raw[g][:, 2:4, 0:256].bitcast(I32), 0)
+        for g in (2, 1, 0):
+            for r in range(1, 4):
+                nc.vector.memset(a_sb[4 * g + r][:, 0 : P * r].bitcast(I32), 0)
+
+        for g in (2, 1, 0):
+            k0 = KP * g
+            nc.sync.dma_start(
+                out=b_raw[g][:, 0:2, :],
+                in_=B[k0 : k0 + 256, k0:N].rearrange("(q e) w -> q e w", e=2),
+            )
+            nc.sync.dma_start(
+                out=b_raw[g][:, 2:4, 256:],
+                in_=B[k0 + 256 : k0 + 512, k0 + 256 : N].rearrange("(q e) w -> q e w", e=2),
+            )
+            for r in range(4):
+                i = 4 * g + r
+                nc.sync.dma_start(out=a_sb[i][:, P * r :], in_=A[P * i : P * i + P, P * i : N])
+
+        ident = const.tile([P, P], F32, name="ident")
+        make_identity(nc, ident[:])
+        mfa = const.tile([P, 2, 64], F32, name="mfa")
+        mfb = const.tile([P, 2, 2, P], F32, name="mfb")
+        nc.gpsimd.memset(mfa[:], -1.0)
+        nc.gpsimd.memset(mfb[:], -1.0)
+        nc.gpsimd.affine_select(
+            out=mfa[:], in_=mfa[:], pattern=[[1, 2], [2, 64]], compare_op=ALU.is_ge,
+            fill=0.0, base=0, channel_multiplier=-1,
+        )
+        nc.gpsimd.affine_select(
+            out=mfb[:], in_=mfb[:], pattern=[[1, 2], [-1, 2], [2, P]], compare_op=ALU.is_ge,
+            fill=0.0, base=0, channel_multiplier=-2,
+        )
+        mi = const.tile([P, 2, 320], I32, name="mi")
+        mw = const.tile([P, 320], I32, name="mw")
+        mask_a = mw[:, 0:64]
+        mask_b = mw[:, 64:320].rearrange("p (e x) -> p e x", e=2)
+
+        def zero_rows_scalar(rows):
+            for i in rows:
+                for lo in range(0, P * i, 1024):
+                    hi = min(P * i, lo + 1024)
+                    nc.scalar.copy(out=o_sb[i][:, lo:hi], in_=o_sb[8][:, 0 : hi - lo])
+
+        def mask_a_blocks(g):
+            for r in range(4):
+                blk = a_sb[4 * g + r][:, P * r : P * r + P].bitcast(I32)
+                nc.vector.tensor_tensor(out=blk, in0=blk, in1=mask_a, op=ALU.bitwise_and)
+
+        def mask_b_blocks(g):
+            for u in range(2):
+                blk = b_raw[g][:, 2 * u : 2 * u + 2, 256 * u : 256 * u + 256].bitcast(I32)
+                nc.vector.tensor_tensor(out=blk, in0=blk, in1=mask_b, op=ALU.bitwise_and)
+
+        def transpose_a(g, c):
+            gaf = ga[slot(g, c)][:].bitcast(F32)
+            for b in range(2):
+                xt = bank([P, 2, 2, P])
+                for q in range(2):
+                    af = a_sb[4 * g + 2 * b + q][:].bitcast(F32)
+                    for u in range(2):
+                        w0 = 256 * (c - g) + P * u
+                        nc.tensor.transpose(xt[:, q, u, :], af[:, w0 : w0 + P], ident[:])
+                nc.scalar.copy(
+                    out=gaf[:, 512 * b : 512 * b + 512].rearrange("p (q i u) -> p q i u", q=2, u=2),
+                    in_=xt[:].rearrange("p q u i -> p q i u"),
+                )
+
+        def quant_a(g, c):
+            s = slot(g, c)
+            nc.vector.quantize_mx(out=a_cod[:, s, :].bitcast(FP8X4), scales=a_scl[:, s, :], in_=ga[s][:])
+
+        def regroup_b(c, j):
+            src = b_raw[c][:, :, KP * (j - c) : KP * (j - c) + KP]
+            nc.vector.tensor_copy(
+                out=gb[slot(c, j)][:].rearrange("p (c i) t -> p c t i", i=4),
+                in_=src.rearrange("p t (c i) -> p c t i", i=4),
+            )
+
+        def quant_b(c, j):
+            s = slot(c, j)
+            nc.vector.quantize_mx(
+                out=b_cod[:, s, :].bitcast(FP8X4), scales=b_scl[:, s, :],
+                in_=gb[s][:].rearrange("p w t -> p (w t)"),
+            )
+
+        def mx(acc, g, r, c, j, off, wid, start, stop):
+            sa = slot(g, c)
+            sb = slot(c, j)
+            rows = slice(P * r, P * r + P)
+            nc.tensor.matmul_mx(
+                out=acc[:, off : off + wid],
+                lhsT=a_cod[:, sa, rows].bitcast(FP8X4), lhsT_scale=a_scl[:, sa, rows],
+                rhs=b_cod[:, sb, off : off + wid].bitcast(FP8X4), rhs_scale=b_scl[:, sb, off : off + wid],
+                start=start, stop=stop,
+            )
+
+        def evac(eng, acc, g, r, j, lo):
+            dst = o_sb[4 * g + r][:, KP * j + lo : KP * j + KP]
+            if eng == "v":
+                nc.vector.tensor_copy(out=dst, in_=acc[:, lo:KP])
+            else:
+                nc.scalar.copy(out=dst, in_=acc[:, lo:KP])
+
+        def diag_tiles(g):
+            for r in range(4):
+                acc = bank([P, KP])
+                for off, wid in PIECES[r]:
+                    mx(acc, g, r, g, g, off, wid, True, True)
+                evac("s", acc, g, r, g, P * r)
+
+        def store(i):
+            nc.sync.dma_start(out=out[P * i : P * i + P, :], in_=o_sb[i][:])
+
+        nc.vector.memset(o_sb[8][:, 0:1024], 0.0)
+        zero_rows_scalar([10, 11])
+        nc.vector.memset(o_sb[9][:, 0:1152], 0.0)
+        nc.vector.tensor_copy(out=mi[:, :, 0:64], in_=mfa[:])
+        nc.vector.tensor_copy(out=mi[:, :, 64:320], in_=mfb[:].rearrange("p h e x -> p h (e x)"))
+        nc.vector.tensor_single_scalar(out=mi[:, 0, :], in_=mi[:, 0, :], scalar=16, op=ALU.logical_shift_right)
+        nc.vector.tensor_single_scalar(out=mi[:, 1, :], in_=mi[:, 1, :], scalar=16, op=ALU.logical_shift_left)
+        nc.vector.tensor_tensor(out=mw[:], in0=mi[:, 0, :], in1=mi[:, 1, :], op=ALU.bitwise_or)
+
+        mask_b_blocks(2)
+        mask_a_blocks(2)
+        transpose_a(2, 2)
+        regroup_b(2, 2)
+        zero_rows_scalar([4, 5, 6, 7])
+        quant_b(2, 2)
+        quant_a(2, 2)
+        diag_tiles(2)
+        for r in range(4):
+            store(8 + r)
+
+        mask_b_blocks(1)
+        regroup_b(1, 1)
+        mask_a_blocks(1)
+        transpose_a(1, 1)
+        transpose_a(1, 2)
+        regroup_b(1, 2)
+        quant_b(1, 1)
+        quant_a(1, 1)
+        diag_tiles(1)
+        zero_rows_scalar([1, 2, 3])
+        quant_b(1, 2)
+        acc12 = {}
+        for r in range(4):
+            acc12[r] = bank([P, KP])
+            mx(acc12[r], 1, r, 1, 2, 0, KP, True, False)
+        quant_a(1, 2)
+        for r in range(4):
+            mx(acc12[r], 1, r, 2, 2, 0, KP, False, True)
+            evac("s", acc12[r], 1, r, 2, 0)
+            store(4 + r)
+
+        mask_b_blocks(0)
+        regroup_b(0, 0)
+        mask_a_blocks(0)
+        for c in range(NG):
+            transpose_a(0, c)
+        regroup_b(0, 1)
+        quant_b(0, 0)
+        quant_a(0, 0)
+        diag_tiles(0)
+        regroup_b(0, 2)
+        quant_b(0, 1)
+        acc01 = {}
+        for r in range(4):
+            acc01[r] = bank([P, KP])
+            mx(acc01[r], 0, r, 0, 1, 0, KP, True, False)
+        quant_a(0, 1)
+        for r in range(4):
+            mx(acc01[r], 0, r, 1, 1, 0, KP, False, True)
+            evac("s", acc01[r], 0, r, 1, 0)
+        acc02 = {}
+        for r in range(4):
+            acc02[r] = bank([P, KP])
+            mx(acc02[r], 0, r, 1, 2, 0, KP, True, False)
+        quant_a(0, 2)
+        for r in range(4):
+            mx(acc02[r], 0, r, 2, 2, 0, KP, False, False)
+        quant_b(0, 2)
+        for r in range(4):
+            mx(acc02[r], 0, r, 0, 2, 0, KP, False, True)
+            evac("v" if r % 2 == 0 else "s", acc02[r], 0, r, 2, 0)
+            store(r)

@@ -39,7 +39,7 @@ def tile_modelnew_kernel(tc, A, B, out):
         o_sb = {}
         for i in range(12):
             a_sb[i] = keep.tile([P, N - KP * (i // 4)], BF16, name="a_sb%d" % i)
-            o_sb[i] = keep.tile([P, N], F32, name="o_sb%d" % i)
+            o_sb[i] = keep.tile([P, N - P * i], F32, name="o_sb%d" % i)
         b_raw = {}
         for c in range(NG):
             b_raw[c] = keep.tile([P, 4, N - KP * c], BF16, name="b_raw%d" % c)
@@ -52,6 +52,12 @@ def tile_modelnew_kernel(tc, A, B, out):
         a_scl = keep.tile([P, 6, KP], U8, name="a_scl", align_bytes=64)
         b_cod = keep.tile([P, 6, KP], U32, name="b_cod", align_bytes=64)
         b_scl = keep.tile([P, 6, KP], U8, name="b_scl", align_bytes=64)
+        zeros = const.tile([P, N - P], F32, name="zeros")
+        ident = const.tile([P, P], F32, name="ident")
+        mf = const.tile([P, 320], F32, name="mf")
+        mw = const.tile([P, 320], I32, name="mw")
+        mask_a = mw[:, 0:64]
+        mask_b = mw[:, 64:320].rearrange("p (e x) -> p e x", e=2)
         banks = [0]
 
         def bank(shape):
@@ -59,13 +65,12 @@ def tile_modelnew_kernel(tc, A, B, out):
             banks[0] = n + 1
             return psum.tile(shape, F32, name="bk%d_%d" % (n % 8, n), tag="bk%d" % (n % 8))
 
-        for g in (2, 1, 0):
-            nc.vector.memset(b_raw[g][:, 2:4, 0:256].bitcast(I32), 0)
-        for g in (2, 1, 0):
-            for r in range(1, 4):
-                nc.vector.memset(a_sb[4 * g + r][:, 0 : P * r].bitcast(I32), 0)
+        def load_a(g):
+            for r in range(4):
+                i = 4 * g + r
+                nc.sync.dma_start(out=a_sb[i][:, P * r :], in_=A[P * i : P * i + P, P * i : N])
 
-        for g in (2, 1, 0):
+        def load_b(g):
             k0 = KP * g
             nc.sync.dma_start(
                 out=b_raw[g][:, 0:2, :],
@@ -75,34 +80,6 @@ def tile_modelnew_kernel(tc, A, B, out):
                 out=b_raw[g][:, 2:4, 256:],
                 in_=B[k0 + 256 : k0 + 512, k0 + 256 : N].rearrange("(q e) w -> q e w", e=2),
             )
-            for r in range(4):
-                i = 4 * g + r
-                nc.sync.dma_start(out=a_sb[i][:, P * r :], in_=A[P * i : P * i + P, P * i : N])
-
-        ident = const.tile([P, P], F32, name="ident")
-        make_identity(nc, ident[:])
-        mfa = const.tile([P, 2, 64], F32, name="mfa")
-        mfb = const.tile([P, 2, 2, P], F32, name="mfb")
-        nc.gpsimd.memset(mfa[:], -1.0)
-        nc.gpsimd.memset(mfb[:], -1.0)
-        nc.gpsimd.affine_select(
-            out=mfa[:], in_=mfa[:], pattern=[[1, 2], [2, 64]], compare_op=ALU.is_ge,
-            fill=0.0, base=0, channel_multiplier=-1,
-        )
-        nc.gpsimd.affine_select(
-            out=mfb[:], in_=mfb[:], pattern=[[1, 2], [-1, 2], [2, P]], compare_op=ALU.is_ge,
-            fill=0.0, base=0, channel_multiplier=-2,
-        )
-        mi = const.tile([P, 2, 320], I32, name="mi")
-        mw = const.tile([P, 320], I32, name="mw")
-        mask_a = mw[:, 0:64]
-        mask_b = mw[:, 64:320].rearrange("p (e x) -> p e x", e=2)
-
-        def zero_rows_scalar(rows):
-            for i in rows:
-                for lo in range(0, P * i, 1024):
-                    hi = min(P * i, lo + 1024)
-                    nc.scalar.copy(out=o_sb[i][:, lo:hi], in_=o_sb[8][:, 0 : hi - lo])
 
         def mask_a_blocks(g):
             for r in range(4):
@@ -158,91 +135,106 @@ def tile_modelnew_kernel(tc, A, B, out):
             )
 
         def evac(eng, acc, g, r, j, lo):
-            dst = o_sb[4 * g + r][:, KP * j + lo : KP * j + KP]
+            i = 4 * g + r
+            dst = o_sb[i][:, KP * j + lo - P * i : KP * j + KP - P * i]
             if eng == "v":
                 nc.vector.tensor_copy(out=dst, in_=acc[:, lo:KP])
             else:
                 nc.scalar.copy(out=dst, in_=acc[:, lo:KP])
 
-        def diag_tiles(g):
+        def diag_tile(g, r, eng):
+            acc = bank([P, KP])
+            for off, wid in PIECES[r]:
+                mx(acc, g, r, g, g, off, wid, True, True)
+            evac(eng, acc, g, r, g, P * r)
+
+        def open_tiles():
+            return [bank([P, KP]) for r in range(4)]
+
+        def passes(accs, g, c, j, start, stop):
             for r in range(4):
-                acc = bank([P, KP])
-                for off, wid in PIECES[r]:
-                    mx(acc, g, r, g, g, off, wid, True, True)
-                evac("s", acc, g, r, g, P * r)
+                mx(accs[r], g, r, c, j, 0, KP, start, stop)
 
         def store(i):
-            nc.sync.dma_start(out=out[P * i : P * i + P, :], in_=o_sb[i][:])
+            nc.sync.dma_start(out=out[P * i : P * i + P, P * i : N], in_=o_sb[i][:])
 
-        nc.vector.memset(o_sb[8][:, 0:1024], 0.0)
-        zero_rows_scalar([10, 11])
-        nc.vector.memset(o_sb[9][:, 0:1152], 0.0)
-        nc.vector.tensor_copy(out=mi[:, :, 0:64], in_=mfa[:])
-        nc.vector.tensor_copy(out=mi[:, :, 64:320], in_=mfb[:].rearrange("p h e x -> p h (e x)"))
-        nc.vector.tensor_single_scalar(out=mi[:, 0, :], in_=mi[:, 0, :], scalar=16, op=ALU.logical_shift_right)
-        nc.vector.tensor_single_scalar(out=mi[:, 1, :], in_=mi[:, 1, :], scalar=16, op=ALU.logical_shift_left)
-        nc.vector.tensor_tensor(out=mw[:], in0=mi[:, 0, :], in1=mi[:, 1, :], op=ALU.bitwise_or)
+        for g in (2, 1, 0):
+            nc.vector.memset(b_raw[g][:, 2:4, 0:256].bitcast(I32), 0)
+        for g in (2, 1, 0):
+            for r in range(1, 4):
+                nc.vector.memset(a_sb[4 * g + r][:, 0 : P * r].bitcast(I32), 0)
+        nc.vector.memset(zeros[:], 0.0)
+        for g in (2, 1, 0):
+            load_a(g)
+            load_b(g)
+        for i in range(11, 0, -1):
+            nc.sync.dma_start(out=out[P * i : P * i + P, 0 : P * i], in_=zeros[:, 0 : P * i])
+        nc.gpsimd.memset(mf[:], -1.0)
+        for lo_hi, fill in ((0, -65536.0), (1, 0.0)):
+            nc.gpsimd.affine_select(
+                out=mf[:, 0:64], in_=mf[:, 0:64], pattern=[[2, 64]], compare_op=ALU.is_ge,
+                fill=fill, base=lo_hi, channel_multiplier=-1,
+            )
+            nc.gpsimd.affine_select(
+                out=mf[:, 64:320], in_=mf[:, 64:320], pattern=[[-1, 2], [2, P]], compare_op=ALU.is_ge,
+                fill=fill, base=lo_hi, channel_multiplier=-2,
+            )
+        make_identity(nc, ident[:])
+        nc.vector.tensor_copy(out=mw[:], in_=mf[:])
 
-        mask_b_blocks(2)
         mask_a_blocks(2)
         transpose_a(2, 2)
+        mask_b_blocks(2)
         regroup_b(2, 2)
-        zero_rows_scalar([4, 5, 6, 7])
+        mask_a_blocks(1)
+        transpose_a(1, 1)
+        transpose_a(1, 2)
         quant_b(2, 2)
         quant_a(2, 2)
-        diag_tiles(2)
         for r in range(4):
+            diag_tile(2, r, "s")
             store(8 + r)
 
         mask_b_blocks(1)
         regroup_b(1, 1)
-        mask_a_blocks(1)
-        transpose_a(1, 1)
-        transpose_a(1, 2)
-        regroup_b(1, 2)
-        quant_b(1, 1)
         quant_a(1, 1)
-        diag_tiles(1)
-        zero_rows_scalar([1, 2, 3])
-        quant_b(1, 2)
-        acc12 = {}
+        regroup_b(1, 2)
+        mask_a_blocks(0)
+        for c in (1, 2, 0):
+            transpose_a(0, c)
+        quant_b(1, 1)
         for r in range(4):
-            acc12[r] = bank([P, KP])
-            mx(acc12[r], 1, r, 1, 2, 0, KP, True, False)
+            diag_tile(1, r, "s")
         quant_a(1, 2)
+        acc12 = open_tiles()
+        passes(acc12, 1, 2, 2, True, False)
+        quant_b(1, 2)
         for r in range(4):
-            mx(acc12[r], 1, r, 2, 2, 0, KP, False, True)
+            mx(acc12[r], 1, r, 1, 2, 0, KP, False, True)
             evac("s", acc12[r], 1, r, 2, 0)
             store(4 + r)
 
-        mask_b_blocks(0)
-        regroup_b(0, 0)
-        mask_a_blocks(0)
-        for c in range(NG):
-            transpose_a(0, c)
-        regroup_b(0, 1)
-        quant_b(0, 0)
-        quant_a(0, 0)
-        diag_tiles(0)
-        regroup_b(0, 2)
-        quant_b(0, 1)
-        acc01 = {}
-        for r in range(4):
-            acc01[r] = bank([P, KP])
-            mx(acc01[r], 0, r, 0, 1, 0, KP, True, False)
         quant_a(0, 1)
-        for r in range(4):
-            mx(acc01[r], 0, r, 1, 1, 0, KP, False, True)
-            evac("s", acc01[r], 0, r, 1, 0)
-        acc02 = {}
-        for r in range(4):
-            acc02[r] = bank([P, KP])
-            mx(acc02[r], 0, r, 1, 2, 0, KP, True, False)
+        acc01 = open_tiles()
+        passes(acc01, 0, 1, 1, True, False)
+        acc02 = open_tiles()
+        passes(acc02, 0, 1, 2, True, False)
+        regroup_b(0, 1)
         quant_a(0, 2)
+        passes(acc02, 0, 2, 2, False, False)
+        regroup_b(0, 2)
+        quant_a(0, 0)
+        quant_b(0, 1)
         for r in range(4):
-            mx(acc02[r], 0, r, 2, 2, 0, KP, False, False)
+            mx(acc01[r], 0, r, 0, 1, 0, KP, False, True)
+            evac("s", acc01[r], 0, r, 1, 0)
+        mask_b_blocks(0)
         quant_b(0, 2)
+        regroup_b(0, 0)
+        quant_b(0, 0)
         for r in range(4):
             mx(acc02[r], 0, r, 0, 2, 0, KP, False, True)
-            evac("v" if r % 2 == 0 else "s", acc02[r], 0, r, 2, 0)
+            evac("s" if r % 2 else "v", acc02[r], 0, r, 2, 0)
+        for r in range(4):
+            diag_tile(0, r, "s" if r % 2 else "v")
             store(r)

@@ -22,6 +22,10 @@ BYTES = 2 * (N * (N + 1) // 2) * 2 + N * N * 4
 PIECES = {0: [(0, 512)], 1: [(128, 128), (256, 256)], 2: [(256, 256)], 3: [(384, 128)]}
 
 
+def o_lo(i):
+    return 0 if i < 8 else P * i
+
+
 def slot(first, second):
     base = {2: 0, 1: 1, 0: 3}
     return base[first] + second - first
@@ -39,7 +43,7 @@ def tile_modelnew_kernel(tc, A, B, out):
         o_sb = {}
         for i in range(12):
             a_sb[i] = keep.tile([P, N - KP * (i // 4)], BF16, name="a_sb%d" % i)
-            o_sb[i] = keep.tile([P, N - P * i], F32, name="o_sb%d" % i)
+            o_sb[i] = keep.tile([P, N - o_lo(i)], F32, name="o_sb%d" % i)
         b_raw = {}
         for c in range(NG):
             b_raw[c] = keep.tile([P, 4, N - KP * c], BF16, name="b_raw%d" % c)
@@ -136,7 +140,7 @@ def tile_modelnew_kernel(tc, A, B, out):
 
         def evac(eng, acc, g, r, j, lo):
             i = 4 * g + r
-            dst = o_sb[i][:, KP * j + lo - P * i : KP * j + KP - P * i]
+            dst = o_sb[i][:, KP * j + lo - o_lo(i) : KP * j + KP - o_lo(i)]
             if eng == "v":
                 nc.vector.tensor_copy(out=dst, in_=acc[:, lo:KP])
             else:
@@ -155,20 +159,25 @@ def tile_modelnew_kernel(tc, A, B, out):
             for r in range(4):
                 mx(accs[r], g, r, c, j, 0, KP, start, stop)
 
-        def store(i):
-            nc.sync.dma_start(out=out[P * i : P * i + P, P * i : N], in_=o_sb[i][:])
+        def zero_prefix(rows):
+            for i in rows:
+                nc.scalar.copy(out=o_sb[i][:, 0 : P * i], in_=zeros[:, 0 : P * i])
 
+        def store(i):
+            nc.sync.dma_start(out=out[P * i : P * i + P, o_lo(i) : N], in_=o_sb[i][:])
+
+        nc.vector.memset(zeros[:], 0.0)
         for g in (2, 1, 0):
             nc.vector.memset(b_raw[g][:, 2:4, 0:256].bitcast(I32), 0)
         for g in (2, 1, 0):
             for r in range(1, 4):
                 nc.vector.memset(a_sb[4 * g + r][:, 0 : P * r].bitcast(I32), 0)
-        nc.vector.memset(zeros[:], 0.0)
         for g in (2, 1, 0):
             load_a(g)
             load_b(g)
-        for i in range(11, 0, -1):
+        for i in range(11, 7, -1):
             nc.sync.dma_start(out=out[P * i : P * i + P, 0 : P * i], in_=zeros[:, 0 : P * i])
+        zero_prefix([4, 5, 6, 7])
         nc.gpsimd.memset(mf[:], -1.0)
         for lo_hi, fill in ((0, -65536.0), (1, 0.0)):
             nc.gpsimd.affine_select(
@@ -194,6 +203,7 @@ def tile_modelnew_kernel(tc, A, B, out):
         for r in range(4):
             diag_tile(2, r, "s")
             store(8 + r)
+        zero_prefix([1, 2, 3])
 
         mask_b_blocks(1)
         regroup_b(1, 1)

@@ -23,7 +23,7 @@ PIECES = {0: [(0, 512)], 1: [(128, 128), (256, 256)], 2: [(256, 256)], 3: [(384,
 
 
 def o_lo(i):
-    return 0 if i < 8 else P * i
+    return 0 if i < 8 else 2 * KP
 
 
 def slot(first, second):
@@ -41,9 +41,13 @@ def tile_modelnew_kernel(tc, A, B, out):
 
         a_sb = {}
         o_sb = {}
+        o_low = keep.tile([P, 4, KP], F32, name="o_low")
         for i in range(12):
             a_sb[i] = keep.tile([P, N - KP * (i // 4)], BF16, name="a_sb%d" % i)
-            o_sb[i] = keep.tile([P, N - o_lo(i)], F32, name="o_sb%d" % i)
+            if i < 8:
+                o_sb[i] = keep.tile([P, N], F32, name="o_sb%d" % i)
+            else:
+                o_sb[i] = o_low[:, i - 8, :]
         b_raw = {}
         for c in range(NG):
             b_raw[c] = keep.tile([P, 4, N - KP * c], BF16, name="b_raw%d" % c)
@@ -56,7 +60,7 @@ def tile_modelnew_kernel(tc, A, B, out):
         a_scl = keep.tile([P, 6, KP], U8, name="a_scl", align_bytes=64)
         b_cod = keep.tile([P, 6, KP], U32, name="b_cod", align_bytes=64)
         b_scl = keep.tile([P, 6, KP], U8, name="b_scl", align_bytes=64)
-        zeros = const.tile([P, N - P], F32, name="zeros")
+        zeros = const.tile([P, 2 * KP], F32, name="zeros")
         ident = const.tile([P, P], F32, name="ident")
         mf = const.tile([P, 320], F32, name="mf")
         mw = const.tile([P, 320], I32, name="mw")
@@ -161,7 +165,7 @@ def tile_modelnew_kernel(tc, A, B, out):
 
         def zero_prefix(rows):
             for i in rows:
-                nc.scalar.copy(out=o_sb[i][:, 0 : P * i], in_=zeros[:, 0 : P * i])
+                nc.scalar.copy(out=o_sb[i][:, 0 : P * i - o_lo(i)], in_=zeros[:, 0 : P * i - o_lo(i)])
 
         def store(i):
             nc.sync.dma_start(out=out[P * i : P * i + P, o_lo(i) : N], in_=o_sb[i][:])
@@ -175,9 +179,11 @@ def tile_modelnew_kernel(tc, A, B, out):
         for g in (2, 1, 0):
             load_a(g)
             load_b(g)
-        for i in range(11, 7, -1):
-            nc.sync.dma_start(out=out[P * i : P * i + P, 0 : P * i], in_=zeros[:, 0 : P * i])
-        zero_prefix([4, 5, 6, 7])
+        nc.sync.dma_start(
+            out=out[2 * KP : N, 0 : 2 * KP].rearrange("(r p) w -> p r w", p=P),
+            in_=zeros[:].unsqueeze(1).to_broadcast([P, 4, 2 * KP]),
+        )
+        zero_prefix([9, 10, 11, 4, 5, 6, 7])
         nc.gpsimd.memset(mf[:], -1.0)
         for lo_hi, fill in ((0, -65536.0), (1, 0.0)):
             nc.gpsimd.affine_select(
@@ -202,7 +208,7 @@ def tile_modelnew_kernel(tc, A, B, out):
         quant_a(2, 2)
         for r in range(4):
             diag_tile(2, r, "s")
-            store(8 + r)
+        nc.sync.dma_start(out=out[2 * KP : N, 2 * KP : N].rearrange("(r p) w -> p r w", p=P), in_=o_low[:])
         zero_prefix([1, 2, 3])
 
         mask_b_blocks(1)

from contextlib import ExitStack

import concourse.mybir as mybir
from concourse.masks import make_identity

FP8X4 = mybir.dt.float8_e4m3fn_x4
BF16 = mybir.dt.bfloat16
F32 = mybir.dt.float32
I32 = mybir.dt.int32
U32 = mybir.dt.uint32
U8 = mybir.dt.uint8
ALU = mybir.AluOpType

N = 1536
P = 128
KP = 512
NG = N // KP

FLOPS = 2 * N * (N + 1) * (N + 2) // 6
BYTES = 2 * (N * (N + 1) // 2) * 2 + N * N * 4

PIECES = {0: [(0, 512)], 1: [(128, 128), (256, 256)], 2: [(256, 256)], 3: [(384, 128)]}


def o_lo(i):
    return 0 if i < 8 else 2 * KP


def slot(first, second):
    base = {2: 0, 1: 1, 0: 3}
    return base[first] + second - first


def tile_modelnew_kernel(tc, A, B, out):
    nc = tc.nc
    with ExitStack() as ctx:
        const = ctx.enter_context(tc.tile_pool(name="const", bufs=1))
        keep = ctx.enter_context(tc.tile_pool(name="keep", bufs=1))
        psum = ctx.enter_context(tc.psum_pool(name="psum", bufs=1))
        ctx.enter_context(tc.manual_schedule())

        a_sb = {}
        o_sb = {}
        o_low = keep.tile([P, 4, KP], F32, name="o_low")
        for i in range(12):
            a_sb[i] = keep.tile([P, N - KP * (i // 4)], BF16, name="a_sb%d" % i)
            if i < 8:
                o_sb[i] = keep.tile([P, N], F32, name="o_sb%d" % i)
            else:
                o_sb[i] = o_low[:, i - 8, :]
        b_raw = {}
        for c in range(NG):
            b_raw[c] = keep.tile([P, 4, N - KP * c], BF16, name="b_raw%d" % c)
        ga = {}
        gb = {}
        for s in range(6):
            ga[s] = keep.tile([P, 4 * KP], BF16, name="ga%d" % s, align_bytes=64)
            gb[s] = keep.tile([P, KP, 4], BF16, name="gb%d" % s, align_bytes=64)
        a_cod = keep.tile([P, 6, KP], U32, name="a_cod", align_bytes=64)
        a_scl = keep.tile([P, 6, KP], U8, name="a_scl", align_bytes=64)
        b_cod = keep.tile([P, 6, KP], U32, name="b_cod", align_bytes=64)
        b_scl = keep.tile([P, 6, KP], U8, name="b_scl", align_bytes=64)
        zeros = const.tile([P, 2 * KP], F32, name="zeros")
        ident = const.tile([P, P], F32, name="ident")
        mf = const.tile([P, 320], F32, name="mf")
        mw = const.tile([P, 320], I32, name="mw")
        mask_a = mw[:, 0:64]
        mask_b = mw[:, 64:320].rearrange("p (e x) -> p e x", e=2)
        banks = [0]

        def bank(shape):
            n = banks[0]
            banks[0] = n + 1
            return psum.tile(shape, F32, name="bk%d_%d" % (n % 8, n), tag="bk%d" % (n % 8))

        def load_a(g):
            for r in range(4):
                i = 4 * g + r
                nc.sync.dma_start(out=a_sb[i][:, P * r :], in_=A[P * i : P * i + P, P * i : N])

        def load_b(g):
            k0 = KP * g
            nc.sync.dma_start(
                out=b_raw[g][:, 0:2, :],
                in_=B[k0 : k0 + 256, k0:N].rearrange("(q e) w -> q e w", e=2),
            )
            nc.sync.dma_start(
                out=b_raw[g][:, 2:4, 256:],
                in_=B[k0 + 256 : k0 + 512, k0 + 256 : N].rearrange("(q e) w -> q e w", e=2),
            )

        def mask_a_blocks(g):
            for r in range(4):
                blk = a_sb[4 * g + r][:, P * r : P * r + P].bitcast(I32)
                nc.vector.tensor_tensor(out=blk, in0=blk, in1=mask_a, op=ALU.bitwise_and)

        def mask_b_blocks(g):
            for u in range(2):
                blk = b_raw[g][:, 2 * u : 2 * u + 2, 256 * u : 256 * u + 256].bitcast(I32)
                nc.vector.tensor_tensor(out=blk, in0=blk, in1=mask_b, op=ALU.bitwise_and)

        def transpose_a(g, c):
            gaf = ga[slot(g, c)][:].bitcast(F32)
            for b in range(2):
                xt = bank([P, 2, 2, P])
                for q in range(2):
                    af = a_sb[4 * g + 2 * b + q][:].bitcast(F32)
                    for u in range(2):
                        w0 = 256 * (c - g) + P * u
                        nc.tensor.transpose(xt[:, q, u, :], af[:, w0 : w0 + P], ident[:])
                nc.scalar.copy(
                    out=gaf[:, 512 * b : 512 * b + 512].rearrange("p (q i u) -> p q i u", q=2, u=2),
                    in_=xt[:].rearrange("p q u i -> p q i u"),
                )

        def quant_a(g, c):
            s = slot(g, c)
            nc.vector.quantize_mx(out=a_cod[:, s, :].bitcast(FP8X4), scales=a_scl[:, s, :], in_=ga[s][:])

        def regroup_b(c, j):
            src = b_raw[c][:, :, KP * (j - c) : KP * (j - c) + KP]
            nc.vector.tensor_copy(
                out=gb[slot(c, j)][:].rearrange("p (c i) t -> p c t i", i=4),
                in_=src.rearrange("p t (c i) -> p c t i", i=4),
            )

        def quant_b(c, j):
            s = slot(c, j)
            nc.vector.quantize_mx(
                out=b_cod[:, s, :].bitcast(FP8X4), scales=b_scl[:, s, :],
                in_=gb[s][:].rearrange("p w t -> p (w t)"),
            )

        def mx(acc, g, r, c, j, off, wid, start, stop):
            sa = slot(g, c)
            sb = slot(c, j)
            rows = slice(P * r, P * r + P)
            nc.tensor.matmul_mx(
                out=acc[:, off : off + wid],
                lhsT=a_cod[:, sa, rows].bitcast(FP8X4), lhsT_scale=a_scl[:, sa, rows],
                rhs=b_cod[:, sb, off : off + wid].bitcast(FP8X4), rhs_scale=b_scl[:, sb, off : off + wid],
                start=start, stop=stop,
            )

        def evac(eng, acc, g, r, j, lo):
            i = 4 * g + r
            dst = o_sb[i][:, KP * j + lo - o_lo(i) : KP * j + KP - o_lo(i)]
            if eng == "v":
                nc.vector.tensor_copy(out=dst, in_=acc[:, lo:KP])
            else:
                nc.scalar.copy(out=dst, in_=acc[:, lo:KP])

        def diag_tile(g, r, eng):
            acc = bank([P, KP])
            for off, wid in PIECES[r]:
                mx(acc, g, r, g, g, off, wid, True, True)
            evac(eng, acc, g, r, g, P * r)

        def open_tiles():
            return [bank([P, KP]) for r in range(4)]

        def passes(accs, g, c, j, start, stop):
            for r in range(4):
                mx(accs[r], g, r, c, j, 0, KP, start, stop)

        def zero_prefix(rows):
            for i in rows:
                nc.scalar.copy(out=o_sb[i][:, 0 : P * i - o_lo(i)], in_=zeros[:, 0 : P * i - o_lo(i)])

        def store(i):
            nc.sync.dma_start(out=out[P * i : P * i + P, o_lo(i) : N], in_=o_sb[i][:])

        nc.vector.memset(zeros[:], 0.0)
        for g in (2, 1, 0):
            nc.vector.memset(b_raw[g][:, 2:4, 0:256].bitcast(I32), 0)
        for g in (2, 1, 0):
            for r in range(1, 4):
                nc.vector.memset(a_sb[4 * g + r][:, 0 : P * r].bitcast(I32), 0)
        for g in (2, 1, 0):
            load_a(g)
            load_b(g)
        nc.sync.dma_start(
            out=out[2 * KP : N, 0 : 2 * KP].rearrange("(r p) w -> p r w", p=P),
            in_=zeros[:].unsqueeze(1).to_broadcast([P, 4, 2 * KP]),
        )
        zero_prefix([9, 10, 11, 4, 5, 6, 7])
        nc.gpsimd.memset(mf[:], -1.0)
        for lo_hi, fill in ((0, -65536.0), (1, 0.0)):
            nc.gpsimd.affine_select(
                out=mf[:, 0:64], in_=mf[:, 0:64], pattern=[[2, 64]], compare_op=ALU.is_ge,
                fill=fill, base=lo_hi, channel_multiplier=-1,
            )
            nc.gpsimd.affine_select(
                out=mf[:, 64:320], in_=mf[:, 64:320], pattern=[[-1, 2], [2, P]], compare_op=ALU.is_ge,
                fill=fill, base=lo_hi, channel_multiplier=-2,
            )
        make_identity(nc, ident[:])
        nc.vector.tensor_copy(out=mw[:], in_=mf[:])

        mask_a_blocks(2)
        transpose_a(2, 2)
        mask_b_blocks(2)
        regroup_b(2, 2)
        mask_a_blocks(1)
        transpose_a(1, 1)
        transpose_a(1, 2)
        quant_b(2, 2)
        quant_a(2, 2)
        for r in range(4):
            diag_tile(2, r, "s")
        nc.sync.dma_start(out=out[2 * KP : N, 2 * KP : N].rearrange("(r p) w -> p r w", p=P), in_=o_low[:])
        zero_prefix([1, 2, 3])

        mask_b_blocks(1)
        regroup_b(1, 1)
        quant_a(1, 1)
        regroup_b(1, 2)
        mask_a_blocks(0)
        for c in (1, 2, 0):
            transpose_a(0, c)
        quant_b(1, 1)
        for r in range(4):
            diag_tile(1, r, "s")
        quant_a(1, 2)
        acc12 = open_tiles()
        passes(acc12, 1, 2, 2, True, False)
        quant_b(1, 2)
        for r in range(4):
            mx(acc12[r], 1, r, 1, 2, 0, KP, False, True)
            evac("s", acc12[r], 1, r, 2, 0)
            store(4 + r)

        quant_a(0, 1)
        acc01 = open_tiles()
        passes(acc01, 0, 1, 1, True, False)
        acc02 = open_tiles()
        passes(acc02, 0, 1, 2, True, False)
        regroup_b(0, 1)
        quant_a(0, 2)
        passes(acc02, 0, 2, 2, False, False)
        regroup_b(0, 2)
        quant_a(0, 0)
        quant_b(0, 1)
        for r in range(4):
            mx(acc01[r], 0, r, 0, 1, 0, KP, False, True)
            evac("s", acc01[r], 0, r, 1, 0)
        mask_b_blocks(0)
        quant_b(0, 2)
        regroup_b(0, 0)
        quant_b(0, 0)
        for r in range(4):
            mx(acc02[r], 0, r, 0, 2, 0, KP, False, True)
            evac("s" if r % 2 else "v", acc02[r], 0, r, 2, 0)
        for r in range(4):
            diag_tile(0, r, "s" if r % 2 else "v")
            store(r)
